import numpy as np
import ml_dtypes


def mxq(x, axis, fmt="e4m3"):
    dtype, down = {"e4m3": (ml_dtypes.float8_e4m3fn, 7), "e5m2": (ml_dtypes.float8_e5m2, 14)}[fmt]
    v = np.moveaxis(np.asarray(x, np.float32).astype(ml_dtypes.bfloat16).astype(np.float64), axis, -1)
    blocks = v.reshape(v.shape[:-1] + (-1, 32))
    amax = np.abs(blocks).max(-1, keepdims=True)
    byte = np.maximum(np.where(amax > 0, np.frexp(amax)[1] - 1 + 127, 0) - down, 1)
    scale = np.exp2(byte - 127.0)
    codes = (blocks / scale).astype(np.float32).astype(dtype).astype(np.float64)
    return np.moveaxis((codes * scale).reshape(v.shape), -1, axis)


WIDE = False


def mx_kscale(k):
    if not WIDE:
        return np.ones(k)
    levels = np.array([10, -10, 5, -5, 0])
    a = np.random.permutation(np.resize(levels, k // 512 * 4)).reshape(k // 512, 4)
    idx = np.arange(k)
    return np.exp2(a[idx // 512, idx % 128 // 32])


BF16 = ml_dtypes.bfloat16


def bf(x):
    return np.asarray(x, np.float32).astype(BF16)


def f64(x):
    return np.asarray(x).astype(np.float64)


B, D, G, S, K, E, H, C1, C2, C3 = 256, 1024, 16, 256, 256, 2, 1024, 8, 64, 128
EPS = 1e-5


def sigmoid(v):
    return 1.0 / (1.0 + np.exp(-v))


def setup_inputs():
    t = mx_kscale(H)
    return {"le": bf(np.maximum(np.random.standard_normal((B, G, S)), 0.0) * 1.25),
            "ew1": bf(np.random.standard_normal((E, H, S)) * 1.2 / np.sqrt(S)),
            "ew2": bf(np.random.standard_normal((E, K, H)) * 3.0 / np.sqrt(H) / t),
            "ebg": bf((1.0 + 0.1 * np.random.standard_normal((E, G, H))) * t),
            "ebb": bf(0.3 * np.random.standard_normal((E, G, H)) * t),
            "ebm": bf(0.3 * np.random.standard_normal((E, G, H))),
            "ebv": bf(0.5 + np.random.uniform(size=(E, G, H)))}


def reference(le, ew1, ew2, ebg, ebb, ebm, ebv):
    u = (f64(le).reshape(B * G, S) @ f64(ew1).transpose(0, 2, 1)).reshape(E, B, G, H)
    gain = f64(ebg) / np.sqrt(f64(ebv) + EPS)
    h = np.maximum((u - f64(ebm)[:, None]) * gain[:, None] + f64(ebb)[:, None], 0.0)
    hq = mxq(h.reshape(E, B * G, H), 2, "e4m3")
    out = (hq @ mxq(f64(ew2), 2, "e4m3").transpose(0, 2, 1)).reshape(E, B, G, K)
    sel = sigmoid(out[0])
    sel = np.clip(1.2 * sel - 0.1, 0.0, 1.0)
    layer_bias = out[E - 1]
    return sel, layer_bias

@@ -1,0 +1,273 @@
+from contextlib import ExitStack
+
+import concourse.bass as bass
+import concourse.mybir as mybir
+import concourse.tile as tile
+from concourse.masks import make_identity
+
+F32 = mybir.dt.float32
+BF16 = mybir.dt.bfloat16
+U32 = mybir.dt.uint32
+U8 = mybir.dt.uint8
+FP8X4 = mybir.dt.float8_e4m3fn_x4
+ACT = mybir.ActivationFunctionType
+ALU = mybir.AluOpType
+
+P = 128
+B, G, S, H, K, E = 256, 16, 256, 1024, 256, 2
+EPS = 1e-5
+FLOPS = 2 * B * G * S * H * E + 2 * B * G * H * K * E
+
+PIN = False
+NU = 32
+V_BANKS = ((1, 0), (3, 0))
+LE_CHUNKS = ((0, 2), (2, 4), (4, 8), (8, 16))
+
+
+def tile_tgnetworkbias_pa_t_kernel(tc, le, ew1, ew2, ebg, ebb, ebm, ebv, out_0, out_1):
+    nc = tc.nc
+    with ExitStack() as ctx:
+        const = ctx.enter_context(tc.tile_pool(name="const", bufs=1))
+        hbp = ctx.enter_context(tc.tile_pool(name="hbp", bufs=3))
+        grp = ctx.enter_context(tc.tile_pool(name="grp", bufs=3))
+        cdp = ctx.enter_context(tc.tile_pool(name="cdp", bufs=6))
+        outp = ctx.enter_context(tc.tile_pool(name="outp", bufs=6))
+        ps1 = ctx.enter_context(tc.psum_pool(name="ps1", bufs=6))
+        ps2 = ctx.enter_context(tc.psum_pool(name="ps2", bufs=2))
+
+        bn_raw = []
+        for i, src in enumerate((ebv, ebg, ebm, ebb)):
+            t = const.tile([P, 256], BF16, name="bnraw%d" % i)
+            nc.sync.dma_start(out=t[:], in_=src.rearrange("e g (cu x) -> (e g cu) x", x=256))
+            bn_raw.append(t)
+        ebv_sb, ebg_sb, ebm_sb, ebb_sb = bn_raw
+
+        le_v = le.rearrange("(bh p) g s -> p bh (g s)", p=P)
+        le_raw = []
+
+        def load_le(ci):
+            g0, g1 = LE_CHUNKS[ci]
+            t = const.tile([P, 2 * (g1 - g0) * S], BF16, name="leraw%d" % ci)
+            nc.sync.dma_start(out=t[:].rearrange("p (bh x) -> p bh x", bh=2), in_=le_v[:, :, g0 * S:g1 * S])
+            le_raw.append(t)
+
+        w1raw = {}
+
+        def load_w1(e, c):
+            t = const.tile([P, 1024], BF16, name="w1raw%d%d" % (e, c))
+            v = ew1[e].rearrange("(cu p e2) s -> p cu (e2 s)", cu=4, p=P, e2=2)
+            nc.sync.dma_start(out=t[:].rearrange("p (u x) -> p u x", u=2), in_=v[:, 2 * c:2 * c + 2, :])
+            w1raw[(e, c)] = t
+
+        w2raw = {}
+
+        def load_w2(e):
+            t = const.tile([P, 2048], BF16, name="w2raw%d" % e)
+            nc.sync.dma_start(out=t[:].rearrange("p (kb h) -> p kb h", kb=2),
+                              in_=ew2[e].rearrange("(kb p) h -> p kb h", p=P))
+            w2raw[e] = t
+
+        load_le(0)
+        load_w1(0, 0)
+        load_w1(0, 1)
+        load_w1(1, 0)
+        load_w1(1, 1)
+        load_w2(0)
+        load_le(1)
+        load_w2(1)
+        load_le(2)
+        load_le(3)
+
+        ident = const.tile([P, P], F32, name="ident")
+        make_identity(nc, ident[:])
+
+        eps_t = const.tile([P, 1], F32, name="eps_t")
+        nc.vector.memset(eps_t[:], EPS)
+        r = const.tile([P, 256], F32, name="r")
+        nc.scalar.activation(out=r[:], in_=ebv_sb[:], func=ACT.Abs_reciprocal_sqrt, bias=eps_t[:, 0:1], scale=1.0)
+        hv = const.tile([P, 256], F32, name="hv")
+        nc.vector.tensor_scalar(out=hv[:], in0=ebv_sb[:], scalar1=EPS, scalar2=-0.5, op0=ALU.add, op1=ALU.mult)
+        w = const.tile([P, 256], F32, name="w")
+        for it in range(2):
+            nc.vector.tensor_tensor(out=w[:], in0=r[:], in1=hv[:], op=ALU.mult)
+            nc.vector.tensor_tensor(out=w[:], in0=w[:], in1=r[:], op=ALU.mult)
+            nc.vector.scalar_tensor_tensor(out=r[:], in0=w[:], scalar=1.5, in1=r[:], op0=ALU.add, op1=ALU.mult)
+        gs = const.tile([P, 512], F32, name="gs")
+        nc.vector.tensor_tensor(out=gs[:, 0:256], in0=ebg_sb[:], in1=r[:], op=ALU.mult)
+        nc.vector.tensor_tensor(out=w[:], in0=ebm_sb[:], in1=gs[:, 0:256], op=ALU.mult)
+        nc.vector.tensor_tensor(out=gs[:, 256:512], in0=ebb_sb[:], in1=w[:], op=ALU.subtract)
+        prm = const.tile([P, 512], F32, name="prm")
+
+        def prm_transposes():
+            pt = ps1.tile([P, 512], F32, name="u")
+            gv = gs[:].rearrange("p (k x e2) -> p k e2 x", k=2, e2=2)
+            for kind in range(2):
+                for e2 in range(2):
+                    o = (kind * 2 + e2) * P
+                    nc.tensor.transpose(pt[:, o:o + P], gv[:, kind, e2, :], ident[:])
+            nc.vector.tensor_copy(out=prm[:], in_=pt[:])
+
+        leT = {}
+
+        def le_transposes(rg, eng):
+            ci = [i for i, (g0, g1) in enumerate(LE_CHUNKS) if g0 <= 2 * rg < g1][0]
+            g0, g1 = LE_CHUNKS[ci]
+            words = le_raw[ci][:].bitcast(F32)
+            pt = ps1.tile([P, 512], F32, name="u")
+            for gi in range(2):
+                for bh in range(2):
+                    o = (bh * (g1 - g0) + 2 * rg + gi - g0) * P
+                    nc.tensor.transpose(pt[:, (gi * 2 + bh) * P:(gi * 2 + bh + 1) * P], words[:, o:o + P], ident[:])
+            t = const.tile([P, 512], F32, name="leT%d" % rg)
+            if eng == "s":
+                nc.scalar.copy(out=t[:], in_=pt[:])
+            else:
+                nc.vector.tensor_copy(out=t[:], in_=pt[:])
+            leT[rg] = t
+
+        w1T = {}
+
+        def w1_transposes(e, c, eng):
+            words = w1raw[(e, c)][:].bitcast(F32)
+            pt = ps1.tile([P, 512], F32, name="u")
+            for j in range(4):
+                nc.tensor.transpose(pt[:, j * P:(j + 1) * P], words[:, j * P:(j + 1) * P], ident[:])
+            t = const.tile([P, 512], F32, name="w1T%d%d" % (e, c))
+            if eng == "s":
+                nc.scalar.copy(out=t[:], in_=pt[:])
+            else:
+                nc.vector.tensor_copy(out=t[:], in_=pt[:])
+            w1T[(e, c)] = t
+
+        w2c = {}
+        w2s = {}
+
+        def w2_prepare(e, eng):
+            words = w2raw[e][:].bitcast(F32)
+            g2 = const.tile([P, 2048], BF16, name="w2g%d" % e, align_bytes=64)
+            g2w = g2[:].bitcast(F32)
+            for c in range(2):
+                pt = ps1.tile([P, 512], F32, name="u")
+                for u in range(2):
+                    for kb in range(2):
+                        o = kb * 512 + c * 256 + u * P
+                        nc.tensor.transpose(pt[:, u * 256 + kb * P:u * 256 + (kb + 1) * P], words[:, o:o + P], ident[:])
+                dst = g2w[:, c * 512:(c + 1) * 512].rearrange("p (k u) -> p k u", u=2)
+                srcv = pt[:].rearrange("p (u k) -> p k u", u=2)
+                if eng == "s":
+                    nc.scalar.copy(out=dst, in_=srcv)
+                else:
+                    nc.vector.tensor_copy(out=dst, in_=srcv)
+            cw = const.tile([P, 512], U32, name="w2c%d" % e, align_bytes=64)
+            sw = const.tile([P, 512], U8, name="w2s%d" % e, align_bytes=64)
+            nc.vector.quantize_mx(out=cw[:].bitcast(FP8X4), scales=sw[:], in_=g2[:])
+            w2c[e] = cw
+            w2s[e] = sw
+
+        hbs = {}
+        grs = {}
+        cds = {}
+        o2s = {}
+        sgs = {}
+
+        def bank(n, j):
+            rg, e, c = n // 4, (n // 2) % 2, n % 2
+            if j == 0:
+                hb_new = hbp.tile([P, 2048], BF16, name="hb")
+                hbs[n] = hb_new
+            hb = hbs[n]
+            u_ps = ps1.tile([P, 512], F32, name="u")
+            wv = w1T[(e, c)][:].bitcast(BF16).rearrange("q (x a) -> q x a", a=2)
+            xv = leT[rg][:].bitcast(BF16).rearrange("q (x a) -> q x a", a=2)
+            for a in range(2):
+                nc.tensor.matmul(u_ps[:], lhsT=wv[:, j * P:(j + 1) * P, a], rhs=xv[:, :, a], start=(a == 0), stop=(a == 1))
+            on_v = (n % 4, j) in V_BANKS
+            for gi in range(2):
+                rho = e * 64 + (2 * rg + gi) * 4 + 2 * c + j // 2
+                cs = (j % 2) * P + rho
+                cb = (2 + j % 2) * P + rho
+                dst = hb[:, j * 512 + gi * 256:j * 512 + (gi + 1) * 256]
+                srcv = u_ps[:, gi * 256:(gi + 1) * 256]
+                if on_v:
+                    nc.vector.tensor_scalar(out=dst, in0=srcv, scalar1=prm[:, cs:cs + 1], scalar2=prm[:, cb:cb + 1],
+                                            op0=ALU.mult, op1=ALU.add)
+                else:
+                    nc.scalar.activation(out=dst, in_=srcv, func=ACT.Relu, bias=prm[:, cb:cb + 1], scale=prm[:, cs:cs + 1])
+
+        def regroup(n):
+            gr = grp.tile([P, 2048], BF16, name="gr", align_bytes=64)
+            dst = gr[:].rearrange("p (c i t) -> p c t i", i=4, t=4)
+            srcv = hbs[n][:].rearrange("p (t c i) -> p c t i", t=4, i=4)
+            nc.vector.tensor_scalar_max(out=dst, in0=srcv, scalar1=0.0)
+            grs[n] = gr
+
+        def quantise(n):
+            cd = cdp.tile([P, 512], U32, name="cd", align_bytes=64)
+            sc = cdp.tile([P, 512], U8, name="sc", align_bytes=64)
+            nc.vector.quantize_mx(out=cd[:].bitcast(FP8X4), scales=sc[:], in_=grs[n][:])
+            cds[n] = (cd, sc)
+
+        def stage2(su):
+            e = su % 2
+            for bh in range(2):
+                o2 = ps2.tile([P, 512], F32, name="o2")
+                for gi in range(2):
+                    for c in range(2):
+                        cd, sc = cds[2 * su + c]
+                        cols = slice(gi * 256 + bh * P, gi * 256 + (bh + 1) * P)
+                        nc.tensor.matmul_mx(
+                            out=o2[:, gi * 256:(gi + 1) * 256],
+                            lhsT=cd[:, cols].bitcast(FP8X4), lhsT_scale=sc[:, cols],
+                            rhs=w2c[e][:, c * 256:(c + 1) * 256].bitcast(FP8X4), rhs_scale=w2s[e][:, c * 256:(c + 1) * 256],
+                            start=(c == 0), stop=(c == 1))
+                o2s[(su, bh)] = o2
+
+        out_v = [o.rearrange("(bh p) g k -> p bh (g k)", p=P) for o in (out_0, out_1)]
+
+        def evac_first(su, bh):
+            sg = outp.tile([P, 512], F32, name="sg")
+            if su % 2 == 0:
+                nc.scalar.activation(out=sg[:], in_=o2s[(su, bh)][:], func=ACT.Sigmoid)
+            else:
+                nc.vector.tensor_copy(out=sg[:], in_=o2s[(su, bh)][:])
+            sgs[(su, bh)] = sg
+
+        def evac_second(su, bh):
+            sg = sgs[(su, bh)]
+            rg = su // 2
+            if su % 2 == 0:
+                nc.vector.tensor_scalar(out=sg[:], in0=sg[:], scalar1=1.2, scalar2=-0.1, op0=ALU.mult, op1=ALU.add)
+                nc.vector.tensor_scalar(out=sg[:], in0=sg[:], scalar1=0.0, scalar2=1.0, op0=ALU.max, op1=ALU.min)
+            nc.sync.dma_start(out=out_v[su % 2][:, bh, rg * 512:(rg + 1) * 512], in_=sg[:])
+
+        le_transposes(0, "s")
+        w1_transposes(0, 0, "s")
+        w1_transposes(0, 1, "s")
+        prm_transposes()
+        w1_transposes(1, 0, "s")
+        w1_transposes(1, 1, "s")
+
+        if PIN:
+            ctx.enter_context(tc.manual_schedule())
+
+        for n in range(NU + 4):
+            su_e = (n - 4) // 2
+            for j in range(4):
+                if n < NU:
+                    if j == 0 and n % 4 == 1 and n // 4 + 1 < 8:
+                        le_transposes(n // 4 + 1, "v")
+                    bank(n, j)
+                if j == 1:
+                    if n >= 4 and su_e < 16:
+                        evac_first(su_e, n % 2)
+                        evac_second(su_e, n % 2)
+                    if 1 <= n <= NU:
+                        quantise(n - 1)
+            if n == 0:
+                w2_prepare(0, "v")
+            if n == 2:
+                w2_prepare(1, "v")
+            if n < NU:
+                regroup(n)
+            if n % 2 == 1 and n >= 3 and (n - 3) // 2 < 16:
+                stage2((n - 3) // 2)

@@ -1,8 +1,6 @@
 from contextlib import ExitStack
 
-import concourse.bass as bass
 import concourse.mybir as mybir
-import concourse.tile as tile
 from concourse.masks import make_identity
 
 F32 = mybir.dt.float32
@@ -20,8 +18,19 @@ FLOPS = 2 * B * G * S * H * E + 2 * B * G * H * K * E
 
 PIN = False
 NU = 32
-V_BANKS = ((1, 0), (3, 0))
 LE_CHUNKS = ((0, 2), (2, 4), (4, 8), (8, 16))
+
+
+def on_vector(n, j):
+    return (n == 0 and j % 2 == 1) or (n > 0 and j == 0 and n % 2 == 1)
+
+
+def copy_engine(hh):
+    return "v"
+
+
+LE_ENG = "s"
+W2_ENG = "v"
 
 
 def tile_tgnetworkbias_pa_t_kernel(tc, le, ew1, ew2, ebg, ebb, ebm, ebv, out_0, out_1):
@@ -30,59 +39,63 @@ def tile_tgnetworkbias_pa_t_kernel(tc, le, ew1, ew2, ebg, ebb, ebm, ebv, out_0, 
         const = ctx.enter_context(tc.tile_pool(name="const", bufs=1))
         hbp = ctx.enter_context(tc.tile_pool(name="hbp", bufs=3))
         grp = ctx.enter_context(tc.tile_pool(name="grp", bufs=3))
-        cdp = ctx.enter_context(tc.tile_pool(name="cdp", bufs=6))
+        cdp = ctx.enter_context(tc.tile_pool(name="cdp", bufs=8))
         outp = ctx.enter_context(tc.tile_pool(name="outp", bufs=6))
         ps1 = ctx.enter_context(tc.psum_pool(name="ps1", bufs=6))
         ps2 = ctx.enter_context(tc.psum_pool(name="ps2", bufs=2))
 
+        if PIN:
+            ctx.enter_context(tc.manual_schedule())
+
+        le_v = le.rearrange("(bh p) g s -> p bh (g s)", p=P)
+        le_raw = {}
+
+        def load_le(q, ci):
+            g0, g1 = LE_CHUNKS[ci]
+            t = const.tile([P, 2 * (g1 - g0) * S], BF16, name="leraw%d" % ci)
+            q.dma_start(out=t[:].rearrange("p (bh x) -> p bh x", bh=2), in_=le_v[:, :, g0 * S:g1 * S])
+            le_raw[ci] = t
+
+        w1raw = {}
+
+        def load_w1(q, e, c):
+            t = const.tile([P, 1024], BF16, name="w1raw%d%d" % (e, c))
+            v = ew1[e].rearrange("(cu p e2) s -> p cu (e2 s)", cu=4, p=P, e2=2)
+            q.dma_start(out=t[:].rearrange("p (u x) -> p u x", u=2), in_=v[:, 2 * c:2 * c + 2, :])
+            w1raw[(e, c)] = t
+
+        w2raw = {}
+
+        def load_w2(q, e):
+            t = const.tile([P, 2048], BF16, name="w2raw%d" % e)
+            q.dma_start(out=t[:].rearrange("p (kb h) -> p kb h", kb=2),
+                        in_=ew2[e].rearrange("(kb p) h -> p kb h", p=P))
+            w2raw[e] = t
+
+        load_le(nc.scalar, 0)
+        load_w1(nc.scalar, 0, 0)
+        load_w1(nc.scalar, 0, 1)
         bn_raw = []
         for i, src in enumerate((ebv, ebg, ebm, ebb)):
             t = const.tile([P, 256], BF16, name="bnraw%d" % i)
             nc.sync.dma_start(out=t[:], in_=src.rearrange("e g (cu x) -> (e g cu) x", x=256))
             bn_raw.append(t)
         ebv_sb, ebg_sb, ebm_sb, ebb_sb = bn_raw
-
-        le_v = le.rearrange("(bh p) g s -> p bh (g s)", p=P)
-        le_raw = []
-
-        def load_le(ci):
-            g0, g1 = LE_CHUNKS[ci]
-            t = const.tile([P, 2 * (g1 - g0) * S], BF16, name="leraw%d" % ci)
-            nc.sync.dma_start(out=t[:].rearrange("p (bh x) -> p bh x", bh=2), in_=le_v[:, :, g0 * S:g1 * S])
-            le_raw.append(t)
-
-        w1raw = {}
-
-        def load_w1(e, c):
-            t = const.tile([P, 1024], BF16, name="w1raw%d%d" % (e, c))
-            v = ew1[e].rearrange("(cu p e2) s -> p cu (e2 s)", cu=4, p=P, e2=2)
-            nc.sync.dma_start(out=t[:].rearrange("p (u x) -> p u x", u=2), in_=v[:, 2 * c:2 * c + 2, :])
-            w1raw[(e, c)] = t
-
-        w2raw = {}
-
-        def load_w2(e):
-            t = const.tile([P, 2048], BF16, name="w2raw%d" % e)
-            nc.sync.dma_start(out=t[:].rearrange("p (kb h) -> p kb h", kb=2),
-                              in_=ew2[e].rearrange("(kb p) h -> p kb h", p=P))
-            w2raw[e] = t
-
-        load_le(0)
-        load_w1(0, 0)
-        load_w1(0, 1)
-        load_w1(1, 0)
-        load_w1(1, 1)
-        load_w2(0)
-        load_le(1)
-        load_w2(1)
-        load_le(2)
-        load_le(3)
+        load_w1(nc.sync, 1, 0)
+        load_w1(nc.sync, 1, 1)
+        load_w2(nc.sync, 0)
+        load_le(nc.sync, 1)
+        load_w2(nc.sync, 1)
+        load_le(nc.sync, 2)
+        load_le(nc.sync, 3)
 
         ident = const.tile([P, P], F32, name="ident")
         make_identity(nc, ident[:])
 
         eps_t = const.tile([P, 1], F32, name="eps_t")
         nc.vector.memset(eps_t[:], EPS)
+        warm = const.tile([P, 1], F32, name="warm")
+        nc.scalar.activation(out=warm[:], in_=eps_t[:], func=ACT.Abs_reciprocal_sqrt)
         r = const.tile([P, 256], F32, name="r")
         nc.scalar.activation(out=r[:], in_=ebv_sb[:], func=ACT.Abs_reciprocal_sqrt, bias=eps_t[:, 0:1], scale=1.0)
         hv = const.tile([P, 256], F32, name="hv")
@@ -97,6 +110,12 @@ def tile_tgnetworkbias_pa_t_kernel(tc, le, ew1, ew2, ebg, ebb, ebm, ebv, out_0, 
         nc.vector.tensor_tensor(out=w[:], in0=ebm_sb[:], in1=gs[:, 0:256], op=ALU.mult)
         nc.vector.tensor_tensor(out=gs[:, 256:512], in0=ebb_sb[:], in1=w[:], op=ALU.subtract)
         prm = const.tile([P, 512], F32, name="prm")
+
+        def copy_out(eng, dst, srcv):
+            if eng == "s":
+                nc.scalar.copy(out=dst, in_=srcv)
+            else:
+                nc.vector.tensor_copy(out=dst, in_=srcv)
 
         def prm_transposes():
             pt = ps1.tile([P, 512], F32, name="u")
@@ -119,10 +138,7 @@ def tile_tgnetworkbias_pa_t_kernel(tc, le, ew1, ew2, ebg, ebb, ebm, ebv, out_0, 
                     o = (bh * (g1 - g0) + 2 * rg + gi - g0) * P
                     nc.tensor.transpose(pt[:, (gi * 2 + bh) * P:(gi * 2 + bh + 1) * P], words[:, o:o + P], ident[:])
             t = const.tile([P, 512], F32, name="leT%d" % rg)
-            if eng == "s":
-                nc.scalar.copy(out=t[:], in_=pt[:])
-            else:
-                nc.vector.tensor_copy(out=t[:], in_=pt[:])
+            copy_out(eng, t[:], pt[:])
             leT[rg] = t
 
         w1T = {}
@@ -133,10 +149,7 @@ def tile_tgnetworkbias_pa_t_kernel(tc, le, ew1, ew2, ebg, ebb, ebm, ebv, out_0, 
             for j in range(4):
                 nc.tensor.transpose(pt[:, j * P:(j + 1) * P], words[:, j * P:(j + 1) * P], ident[:])
             t = const.tile([P, 512], F32, name="w1T%d%d" % (e, c))
-            if eng == "s":
-                nc.scalar.copy(out=t[:], in_=pt[:])
-            else:
-                nc.vector.tensor_copy(out=t[:], in_=pt[:])
+            copy_out(eng, t[:], pt[:])
             w1T[(e, c)] = t
 
         w2c = {}
@@ -152,43 +165,44 @@ def tile_tgnetworkbias_pa_t_kernel(tc, le, ew1, ew2, ebg, ebb, ebm, ebv, out_0, 
                     for kb in range(2):
                         o = kb * 512 + c * 256 + u * P
                         nc.tensor.transpose(pt[:, u * 256 + kb * P:u * 256 + (kb + 1) * P], words[:, o:o + P], ident[:])
-                dst = g2w[:, c * 512:(c + 1) * 512].rearrange("p (k u) -> p k u", u=2)
-                srcv = pt[:].rearrange("p (u k) -> p k u", u=2)
-                if eng == "s":
-                    nc.scalar.copy(out=dst, in_=srcv)
-                else:
-                    nc.vector.tensor_copy(out=dst, in_=srcv)
+                copy_out(eng, g2w[:, c * 512:(c + 1) * 512].rearrange("p (k u) -> p k u", u=2),
+                         pt[:].rearrange("p (u k) -> p k u", u=2))
             cw = const.tile([P, 512], U32, name="w2c%d" % e, align_bytes=64)
             sw = const.tile([P, 512], U8, name="w2s%d" % e, align_bytes=64)
             nc.vector.quantize_mx(out=cw[:].bitcast(FP8X4), scales=sw[:], in_=g2[:])
             w2c[e] = cw
             w2s[e] = sw
 
+        ups = {}
         hbs = {}
         grs = {}
         cds = {}
         o2s = {}
         sgs = {}
 
-        def bank(n, j):
+        def bank_pe(n, j):
             rg, e, c = n // 4, (n // 2) % 2, n % 2
-            if j == 0:
-                hb_new = hbp.tile([P, 2048], BF16, name="hb")
-                hbs[n] = hb_new
-            hb = hbs[n]
             u_ps = ps1.tile([P, 512], F32, name="u")
             wv = w1T[(e, c)][:].bitcast(BF16).rearrange("q (x a) -> q x a", a=2)
             xv = leT[rg][:].bitcast(BF16).rearrange("q (x a) -> q x a", a=2)
             for a in range(2):
                 nc.tensor.matmul(u_ps[:], lhsT=wv[:, j * P:(j + 1) * P, a], rhs=xv[:, :, a], start=(a == 0), stop=(a == 1))
-            on_v = (n % 4, j) in V_BANKS
+            ups[(n, j)] = u_ps
+
+        def bank_bn(n, j):
+            rg, e, c = n // 4, (n // 2) % 2, n % 2
+            if j == 0:
+                hb_new = hbp.tile([P, 2048], BF16, name="hb")
+                hbs[n] = hb_new
+            hb = hbs[n]
+            u_ps = ups[(n, j)]
             for gi in range(2):
                 rho = e * 64 + (2 * rg + gi) * 4 + 2 * c + j // 2
                 cs = (j % 2) * P + rho
                 cb = (2 + j % 2) * P + rho
                 dst = hb[:, j * 512 + gi * 256:j * 512 + (gi + 1) * 256]
                 srcv = u_ps[:, gi * 256:(gi + 1) * 256]
-                if on_v:
+                if on_vector(n, j):
                     nc.vector.tensor_scalar(out=dst, in0=srcv, scalar1=prm[:, cs:cs + 1], scalar2=prm[:, cb:cb + 1],
                                             op0=ALU.mult, op1=ALU.add)
                 else:
@@ -207,33 +221,34 @@ def tile_tgnetworkbias_pa_t_kernel(tc, le, ew1, ew2, ebg, ebb, ebm, ebv, out_0, 
             nc.vector.quantize_mx(out=cd[:].bitcast(FP8X4), scales=sc[:], in_=grs[n][:])
             cds[n] = (cd, sc)
 
-        def stage2(su):
+        def stage2(hh):
+            su, bh = hh // 2, hh % 2
             e = su % 2
-            for bh in range(2):
-                o2 = ps2.tile([P, 512], F32, name="o2")
-                for gi in range(2):
-                    for c in range(2):
-                        cd, sc = cds[2 * su + c]
-                        cols = slice(gi * 256 + bh * P, gi * 256 + (bh + 1) * P)
-                        nc.tensor.matmul_mx(
-                            out=o2[:, gi * 256:(gi + 1) * 256],
-                            lhsT=cd[:, cols].bitcast(FP8X4), lhsT_scale=sc[:, cols],
-                            rhs=w2c[e][:, c * 256:(c + 1) * 256].bitcast(FP8X4), rhs_scale=w2s[e][:, c * 256:(c + 1) * 256],
-                            start=(c == 0), stop=(c == 1))
-                o2s[(su, bh)] = o2
+            o2 = ps2.tile([P, 512], F32, name="o2")
+            for gi in range(2):
+                for c in range(2):
+                    cd, sc = cds[2 * su + c]
+                    cols = slice(gi * 256 + bh * P, gi * 256 + (bh + 1) * P)
+                    nc.tensor.matmul_mx(
+                        out=o2[:, gi * 256:(gi + 1) * 256],
+                        lhsT=cd[:, cols].bitcast(FP8X4), lhsT_scale=sc[:, cols],
+                        rhs=w2c[e][:, c * 256:(c + 1) * 256].bitcast(FP8X4), rhs_scale=w2s[e][:, c * 256:(c + 1) * 256],
+                        start=(c == 0), stop=(c == 1))
+            o2s[hh] = o2
 
         out_v = [o.rearrange("(bh p) g k -> p bh (g k)", p=P) for o in (out_0, out_1)]
 
-        def evac_first(su, bh):
+        def evac_first(hh):
             sg = outp.tile([P, 512], F32, name="sg")
-            if su % 2 == 0:
-                nc.scalar.activation(out=sg[:], in_=o2s[(su, bh)][:], func=ACT.Sigmoid)
+            if (hh // 2) % 2 == 0:
+                nc.scalar.activation(out=sg[:], in_=o2s[hh][:], func=ACT.Sigmoid)
             else:
-                nc.vector.tensor_copy(out=sg[:], in_=o2s[(su, bh)][:])
-            sgs[(su, bh)] = sg
+                copy_out(copy_engine(hh), sg[:], o2s[hh][:])
+            sgs[hh] = sg
 
-        def evac_second(su, bh):
-            sg = sgs[(su, bh)]
+        def evac_second(hh):
+            sg = sgs[hh]
+            su, bh = hh // 2, hh % 2
             rg = su // 2
             if su % 2 == 0:
                 nc.vector.tensor_scalar(out=sg[:], in0=sg[:], scalar1=1.2, scalar2=-0.1, op0=ALU.mult, op1=ALU.add)
@@ -242,32 +257,38 @@ def tile_tgnetworkbias_pa_t_kernel(tc, le, ew1, ew2, ebg, ebb, ebm, ebv, out_0, 
 
         le_transposes(0, "s")
         w1_transposes(0, 0, "s")
+        bank_pe(0, 0)
+        bank_pe(0, 1)
         w1_transposes(0, 1, "s")
         prm_transposes()
-        w1_transposes(1, 0, "s")
-        w1_transposes(1, 1, "s")
-
-        if PIN:
-            ctx.enter_context(tc.manual_schedule())
+        nc.scalar.activation(out=warm[:], in_=eps_t[:], func=ACT.Sigmoid)
+        bank_pe(0, 2)
+        bank_pe(0, 3)
+        for j in range(4):
+            bank_bn(0, j)
 
         for n in range(NU + 4):
-            su_e = (n - 4) // 2
             for j in range(4):
-                if n < NU:
-                    if j == 0 and n % 4 == 1 and n // 4 + 1 < 8:
-                        le_transposes(n // 4 + 1, "v")
-                    bank(n, j)
-                if j == 1:
-                    if n >= 4 and su_e < 16:
-                        evac_first(su_e, n % 2)
-                        evac_second(su_e, n % 2)
-                    if 1 <= n <= NU:
-                        quantise(n - 1)
-            if n == 0:
-                w2_prepare(0, "v")
-            if n == 2:
-                w2_prepare(1, "v")
-            if n < NU:
-                regroup(n)
-            if n % 2 == 1 and n >= 3 and (n - 3) // 2 < 16:
-                stage2((n - 3) // 2)
+                if (n, j) == (1, 2):
+                    w1_transposes(1, 0, "s")
+                    w1_transposes(1, 1, "s")
+                if (n, j) == (2, 2):
+                    w2_prepare(0, W2_ENG)
+                if (n, j) == (4, 2):
+                    w2_prepare(1, W2_ENG)
+                if j == 0 and n % 4 == 1 and n // 4 + 1 < 8:
+                    le_transposes(n // 4 + 1, LE_ENG)
+                if 1 <= n < NU:
+                    bank_pe(n, j)
+                    bank_bn(n, j)
+                if j == 0:
+                    if 0 <= n - 4 < NU:
+                        evac_first(n - 4)
+                    if 0 <= n - 1 < NU:
+                        regroup(n - 1)
+                if j == 1 and 0 <= n - 1 < NU:
+                    quantise(n - 1)
+                if j == 2 and 0 <= n - 4 < NU:
+                    evac_second(n - 4)
+                if j == 3 and 0 <= n - 3 < NU:
+                    stage2(n - 3)

@@ -17,7 +17,11 @@ EPS = 1e-5
 FLOPS = 2 * B * G * S * H * E + 2 * B * G * H * K * E
 
 PIN = False
-NU = 32
+SPREAD = True
+FULL = [(rg, e, (0, 1)) for rg in range(8) for e in range(2)]
+GROUPS = FULL[:-1] + [(7, 1, (0,)), (7, 1, (1,))] if False else FULL
+NG = len(GROUPS)
+NU = 2 * NG
 LE_CHUNKS = ((0, 2), (2, 4), (4, 8), (8, 16))
 
 
@@ -117,14 +121,36 @@ def tile_tgnetworkbias_pa_t_kernel(tc, le, ew1, ew2, ebg, ebb, ebm, ebv, out_0, 
             else:
                 nc.vector.tensor_copy(out=dst, in_=srcv)
 
+        jobs = []
+        cursor = {"next": 0}
+
+        def run_one_step():
+            if cursor["next"] < len(jobs):
+                jobs[cursor["next"]]()
+                cursor["next"] = cursor["next"] + 1
+
+        def flush_steps():
+            for k in range(len(jobs) - cursor["next"]):
+                run_one_step()
+
+        def add_job(sources, finish):
+            box = {}
+
+            def step(i):
+                if i == 0:
+                    pt_new = ps1.tile([P, 512], F32, name="u")
+                    box["pt"] = pt_new
+                nc.tensor.transpose(box["pt"][:, i * P:(i + 1) * P], sources[i], ident[:])
+                if i == 3:
+                    finish(box["pt"])
+
+            for i in range(4):
+                jobs.append(lambda i=i: step(i))
+
         def prm_transposes():
-            pt = ps1.tile([P, 512], F32, name="u")
             gv = gs[:].rearrange("p (k x e2) -> p k e2 x", k=2, e2=2)
-            for kind in range(2):
-                for e2 in range(2):
-                    o = (kind * 2 + e2) * P
-                    nc.tensor.transpose(pt[:, o:o + P], gv[:, kind, e2, :], ident[:])
-            nc.vector.tensor_copy(out=prm[:], in_=pt[:])
+            add_job([gv[:, kind, e2, :] for kind in range(2) for e2 in range(2)],
+                    lambda pt: nc.vector.tensor_copy(out=prm[:], in_=pt[:]))
 
         leT = {}
 
@@ -132,24 +158,17 @@ def tile_tgnetworkbias_pa_t_kernel(tc, le, ew1, ew2, ebg, ebb, ebm, ebv, out_0, 
             ci = [i for i, (g0, g1) in enumerate(LE_CHUNKS) if g0 <= 2 * rg < g1][0]
             g0, g1 = LE_CHUNKS[ci]
             words = le_raw[ci][:].bitcast(F32)
-            pt = ps1.tile([P, 512], F32, name="u")
-            for gi in range(2):
-                for bh in range(2):
-                    o = (bh * (g1 - g0) + 2 * rg + gi - g0) * P
-                    nc.tensor.transpose(pt[:, (gi * 2 + bh) * P:(gi * 2 + bh + 1) * P], words[:, o:o + P], ident[:])
+            offs = [(bh * (g1 - g0) + 2 * rg + gi - g0) * P for gi in range(2) for bh in range(2)]
             t = const.tile([P, 512], F32, name="leT%d" % rg)
-            copy_out(eng, t[:], pt[:])
+            add_job([words[:, o:o + P] for o in offs], lambda pt: copy_out(eng, t[:], pt[:]))
             leT[rg] = t
 
         w1T = {}
 
         def w1_transposes(e, c, eng):
             words = w1raw[(e, c)][:].bitcast(F32)
-            pt = ps1.tile([P, 512], F32, name="u")
-            for j in range(4):
-                nc.tensor.transpose(pt[:, j * P:(j + 1) * P], words[:, j * P:(j + 1) * P], ident[:])
             t = const.tile([P, 512], F32, name="w1T%d%d" % (e, c))
-            copy_out(eng, t[:], pt[:])
+            add_job([words[:, j * P:(j + 1) * P] for j in range(4)], lambda pt: copy_out(eng, t[:], pt[:]))
             w1T[(e, c)] = t
 
         w2c = {}
@@ -159,17 +178,18 @@ def tile_tgnetworkbias_pa_t_kernel(tc, le, ew1, ew2, ebg, ebb, ebm, ebv, out_0, 
             words = w2raw[e][:].bitcast(F32)
             g2 = const.tile([P, 2048], BF16, name="w2g%d" % e, align_bytes=64)
             g2w = g2[:].bitcast(F32)
-            for c in range(2):
-                pt = ps1.tile([P, 512], F32, name="u")
-                for u in range(2):
-                    for kb in range(2):
-                        o = kb * 512 + c * 256 + u * P
-                        nc.tensor.transpose(pt[:, u * 256 + kb * P:u * 256 + (kb + 1) * P], words[:, o:o + P], ident[:])
-                copy_out(eng, g2w[:, c * 512:(c + 1) * 512].rearrange("p (k u) -> p k u", u=2),
-                         pt[:].rearrange("p (u k) -> p k u", u=2))
             cw = const.tile([P, 512], U32, name="w2c%d" % e, align_bytes=64)
             sw = const.tile([P, 512], U8, name="w2s%d" % e, align_bytes=64)
-            nc.vector.quantize_mx(out=cw[:].bitcast(FP8X4), scales=sw[:], in_=g2[:])
+
+            def finish(c, pt):
+                copy_out(eng, g2w[:, c * 512:(c + 1) * 512].rearrange("p (k u) -> p k u", u=2),
+                         pt[:].rearrange("p (u k) -> p k u", u=2))
+                if c == 1:
+                    nc.vector.quantize_mx(out=cw[:].bitcast(FP8X4), scales=sw[:], in_=g2[:])
+
+            for c in range(2):
+                add_job([words[:, kb * 512 + c * 256 + u * P:kb * 512 + c * 256 + (u + 1) * P] for u in range(2) for kb in range(2)],
+                        lambda pt, c=c: finish(c, pt))
             w2c[e] = cw
             w2s[e] = sw
 
@@ -181,27 +201,34 @@ def tile_tgnetworkbias_pa_t_kernel(tc, le, ew1, ew2, ebg, ebb, ebm, ebv, out_0, 
         sgs = {}
 
         def bank_pe(n, j):
-            rg, e, c = n // 4, (n // 2) % 2, n % 2
+            rg, e, gis = GROUPS[n // 2]
+            c = n % 2
+            wd = 256 * len(gis)
             u_ps = ps1.tile([P, 512], F32, name="u")
             wv = w1T[(e, c)][:].bitcast(BF16).rearrange("q (x a) -> q x a", a=2)
             xv = leT[rg][:].bitcast(BF16).rearrange("q (x a) -> q x a", a=2)
             for a in range(2):
-                nc.tensor.matmul(u_ps[:], lhsT=wv[:, j * P:(j + 1) * P, a], rhs=xv[:, :, a], start=(a == 0), stop=(a == 1))
+                nc.tensor.matmul(u_ps[:, 0:wd], lhsT=wv[:, j * P:(j + 1) * P, a], rhs=xv[:, gis[0] * 256:gis[0] * 256 + wd, a],
+                                 start=(a == 0), stop=(a == 1))
+                if SPREAD:
+                    run_one_step()
             ups[(n, j)] = u_ps
 
         def bank_bn(n, j):
-            rg, e, c = n // 4, (n // 2) % 2, n % 2
+            rg, e, gis = GROUPS[n // 2]
+            c = n % 2
+            wd = 256 * len(gis)
             if j == 0:
                 hb_new = hbp.tile([P, 2048], BF16, name="hb")
                 hbs[n] = hb_new
             hb = hbs[n]
             u_ps = ups[(n, j)]
-            for gi in range(2):
+            for i, gi in enumerate(gis):
                 rho = e * 64 + (2 * rg + gi) * 4 + 2 * c + j // 2
                 cs = (j % 2) * P + rho
                 cb = (2 + j % 2) * P + rho
-                dst = hb[:, j * 512 + gi * 256:j * 512 + (gi + 1) * 256]
-                srcv = u_ps[:, gi * 256:(gi + 1) * 256]
+                dst = hb[:, j * wd + i * 256:j * wd + (i + 1) * 256]
+                srcv = u_ps[:, i * 256:(i + 1) * 256]
                 if on_vector(n, j):
                     nc.vector.tensor_scalar(out=dst, in0=srcv, scalar1=prm[:, cs:cs + 1], scalar2=prm[:, cb:cb + 1],
                                             op0=ALU.mult, op1=ALU.add)
@@ -209,23 +236,25 @@ def tile_tgnetworkbias_pa_t_kernel(tc, le, ew1, ew2, ebg, ebb, ebm, ebv, out_0, 
                     nc.scalar.activation(out=dst, in_=srcv, func=ACT.Relu, bias=prm[:, cb:cb + 1], scale=prm[:, cs:cs + 1])
 
         def regroup(n):
+            wd = 256 * len(GROUPS[n // 2][2])
             gr = grp.tile([P, 2048], BF16, name="gr", align_bytes=64)
-            dst = gr[:].rearrange("p (c i t) -> p c t i", i=4, t=4)
-            srcv = hbs[n][:].rearrange("p (t c i) -> p c t i", t=4, i=4)
+            dst = gr[:, 0:4 * wd].rearrange("p (c i t) -> p c t i", i=4, t=4)
+            srcv = hbs[n][:, 0:4 * wd].rearrange("p (t c i) -> p c t i", t=4, i=4)
             nc.vector.tensor_scalar_max(out=dst, in0=srcv, scalar1=0.0)
             grs[n] = gr
 
         def quantise(n):
             cd = cdp.tile([P, 512], U32, name="cd", align_bytes=64)
             sc = cdp.tile([P, 512], U8, name="sc", align_bytes=64)
-            nc.vector.quantize_mx(out=cd[:].bitcast(FP8X4), scales=sc[:], in_=grs[n][:])
+            wd = 256 * len(GROUPS[n // 2][2])
+            nc.vector.quantize_mx(out=cd[:, 0:wd].bitcast(FP8X4), scales=sc[:, 0:wd], in_=grs[n][:, 0:4 * wd])
             cds[n] = (cd, sc)
 
         def stage2(hh):
             su, bh = hh // 2, hh % 2
-            e = su % 2
+            rg, e, gis = GROUPS[su]
             o2 = ps2.tile([P, 512], F32, name="o2")
-            for gi in range(2):
+            for gi in range(len(gis)):
                 for c in range(2):
                     cd, sc = cds[2 * su + c]
                     cols = slice(gi * 256 + bh * P, gi * 256 + (bh + 1) * P)
@@ -240,44 +269,68 @@ def tile_tgnetworkbias_pa_t_kernel(tc, le, ew1, ew2, ebg, ebb, ebm, ebv, out_0, 
 
         def evac_first(hh):
             sg = outp.tile([P, 512], F32, name="sg")
-            if (hh // 2) % 2 == 0:
-                nc.scalar.activation(out=sg[:], in_=o2s[hh][:], func=ACT.Sigmoid)
+            rg, e, gis = GROUPS[hh // 2]
+            wd = 256 * len(gis)
+            if e == 0:
+                nc.scalar.activation(out=sg[:, 0:wd], in_=o2s[hh][:, 0:wd], func=ACT.Sigmoid)
             else:
-                copy_out(copy_engine(hh), sg[:], o2s[hh][:])
+                copy_out(copy_engine(hh), sg[:, 0:wd], o2s[hh][:, 0:wd])
             sgs[hh] = sg
 
         def evac_second(hh):
             sg = sgs[hh]
             su, bh = hh // 2, hh % 2
-            rg = su // 2
-            if su % 2 == 0:
-                nc.vector.tensor_scalar(out=sg[:], in0=sg[:], scalar1=1.2, scalar2=-0.1, op0=ALU.mult, op1=ALU.add)
-                nc.vector.tensor_scalar(out=sg[:], in0=sg[:], scalar1=0.0, scalar2=1.0, op0=ALU.max, op1=ALU.min)
-            nc.sync.dma_start(out=out_v[su % 2][:, bh, rg * 512:(rg + 1) * 512], in_=sg[:])
+            rg, e, gis = GROUPS[su]
+            wd = 256 * len(gis)
+            if e == 0:
+                nc.vector.tensor_scalar(out=sg[:, 0:wd], in0=sg[:, 0:wd], scalar1=1.2, scalar2=-0.1, op0=ALU.mult, op1=ALU.add)
+                nc.vector.tensor_scalar(out=sg[:, 0:wd], in0=sg[:, 0:wd], scalar1=0.0, scalar2=1.0, op0=ALU.max, op1=ALU.min)
+            o = rg * 512 + gis[0] * 256
+            nc.sync.dma_start(out=out_v[e][:, bh, o:o + wd], in_=sg[:, 0:wd])
 
         le_transposes(0, "s")
         w1_transposes(0, 0, "s")
-        bank_pe(0, 0)
-        bank_pe(0, 1)
+        flush_steps()
         w1_transposes(0, 1, "s")
         prm_transposes()
+        if not SPREAD:
+            bank_pe(0, 0)
+            bank_pe(0, 1)
+            flush_steps()
+            bank_pe(0, 2)
+            bank_pe(0, 3)
+        else:
+            for j in range(4):
+                bank_pe(0, j)
         nc.scalar.activation(out=warm[:], in_=eps_t[:], func=ACT.Sigmoid)
-        bank_pe(0, 2)
-        bank_pe(0, 3)
         for j in range(4):
             bank_bn(0, j)
 
         for n in range(NU + 4):
             for j in range(4):
-                if (n, j) == (1, 2):
-                    w1_transposes(1, 0, "s")
-                    w1_transposes(1, 1, "s")
-                if (n, j) == (2, 2):
-                    w2_prepare(0, W2_ENG)
-                if (n, j) == (4, 2):
-                    w2_prepare(1, W2_ENG)
-                if j == 0 and n % 4 == 1 and n // 4 + 1 < 8:
-                    le_transposes(n // 4 + 1, LE_ENG)
+                if SPREAD:
+                    if (n, j) == (1, 0):
+                        w1_transposes(1, 0, "s")
+                        w1_transposes(1, 1, "s")
+                    if (n, j) == (2, 0):
+                        w2_prepare(0, W2_ENG)
+                    if (n, j) == (3, 0):
+                        le_transposes(1, LE_ENG)
+                    if (n, j) == (4, 0):
+                        w2_prepare(1, W2_ENG)
+                    if j == 0 and n % 4 == 1 and 2 <= n // 4 + 1 < 8 and n < 32:
+                        le_transposes(n // 4 + 1, LE_ENG)
+                else:
+                    if (n, j) == (1, 2):
+                        w1_transposes(1, 0, "s")
+                        w1_transposes(1, 1, "s")
+                    if (n, j) == (2, 2):
+                        w2_prepare(0, W2_ENG)
+                    if (n, j) == (4, 2):
+                        w2_prepare(1, W2_ENG)
+                    if j == 0 and n % 4 == 1 and n // 4 + 1 < 8 and n < 32:
+                        le_transposes(n // 4 + 1, LE_ENG)
+                    flush_steps()
                 if 1 <= n < NU:
                     bank_pe(n, j)
                     bank_bn(n, j)

@@ -26,7 +26,7 @@ LE_CHUNKS = ((0, 2), (2, 4), (4, 8), (8, 16))
 
 
 def on_vector(n, j):
-    return (n == 0 and j % 2 == 1) or (n > 0 and j == 0 and n % 2 == 1)
+    return (n == 0 and j % 2 == 1) or (n > 0 and j == 0 and n % 4 != 0)
 
 
 def copy_engine(hh):

@@ -26,7 +26,7 @@ LE_CHUNKS = ((0, 2), (2, 4), (4, 8), (8, 16))
 
 
 def on_vector(n, j):
-    return (n == 0 and j % 2 == 1) or (n > 0 and j == 0 and n % 4 != 0)
+    return (n == 0 and j % 2 == 1) or (n > 0 and j == 0 and n % 4 < 2)
 
 
 def copy_engine(hh):
@@ -44,7 +44,7 @@ def tile_tgnetworkbias_pa_t_kernel(tc, le, ew1, ew2, ebg, ebb, ebm, ebv, out_0, 
         hbp = ctx.enter_context(tc.tile_pool(name="hbp", bufs=3))
         grp = ctx.enter_context(tc.tile_pool(name="grp", bufs=3))
         cdp = ctx.enter_context(tc.tile_pool(name="cdp", bufs=8))
-        outp = ctx.enter_context(tc.tile_pool(name="outp", bufs=6))
+        outp = ctx.enter_context(tc.tile_pool(name="outp", bufs=8))
         ps1 = ctx.enter_context(tc.psum_pool(name="ps1", bufs=6))
         ps2 = ctx.enter_context(tc.psum_pool(name="ps2", bufs=2))
 
@@ -277,16 +277,20 @@ def tile_tgnetworkbias_pa_t_kernel(tc, le, ew1, ew2, ebg, ebb, ebm, ebv, out_0, 
                 copy_out(copy_engine(hh), sg[:, 0:wd], o2s[hh][:, 0:wd])
             sgs[hh] = sg
 
-        def evac_second(hh):
+        def clip_first(hh):
             sg = sgs[hh]
+            nc.vector.tensor_scalar(out=sg[:], in0=sg[:], scalar1=1.2, scalar2=-0.1, op0=ALU.mult, op1=ALU.add)
+
+        def clip_second(hh):
+            sg = sgs[hh]
+            nc.vector.tensor_scalar(out=sg[:], in0=sg[:], scalar1=0.0, scalar2=1.0, op0=ALU.max, op1=ALU.min)
+
+        def store(hh):
             su, bh = hh // 2, hh % 2
             rg, e, gis = GROUPS[su]
             wd = 256 * len(gis)
-            if e == 0:
-                nc.vector.tensor_scalar(out=sg[:, 0:wd], in0=sg[:, 0:wd], scalar1=1.2, scalar2=-0.1, op0=ALU.mult, op1=ALU.add)
-                nc.vector.tensor_scalar(out=sg[:, 0:wd], in0=sg[:, 0:wd], scalar1=0.0, scalar2=1.0, op0=ALU.max, op1=ALU.min)
             o = rg * 512 + gis[0] * 256
-            nc.sync.dma_start(out=out_v[e][:, bh, o:o + wd], in_=sg[:, 0:wd])
+            nc.sync.dma_start(out=out_v[e][:, bh, o:o + wd], in_=sgs[hh][:, 0:wd])
 
         le_transposes(0, "s")
         w1_transposes(0, 0, "s")
@@ -306,7 +310,7 @@ def tile_tgnetworkbias_pa_t_kernel(tc, le, ew1, ew2, ebg, ebb, ebm, ebv, out_0, 
         for j in range(4):
             bank_bn(0, j)
 
-        for n in range(NU + 4):
+        for n in range(NU + 8):
             for j in range(4):
                 if SPREAD:
                     if (n, j) == (1, 0):
@@ -331,17 +335,26 @@ def tile_tgnetworkbias_pa_t_kernel(tc, le, ew1, ew2, ebg, ebb, ebm, ebv, out_0, 
                     if j == 0 and n % 4 == 1 and n // 4 + 1 < 8 and n < 32:
                         le_transposes(n // 4 + 1, LE_ENG)
                     flush_steps()
+                if j == 0 and 0 <= n - 1 < NU:
+                    regroup(n - 1)
                 if 1 <= n < NU:
                     bank_pe(n, j)
                     bank_bn(n, j)
                 if j == 0:
-                    if 0 <= n - 4 < NU:
-                        evac_first(n - 4)
+                    hh = n - 4
+                    if 0 <= hh < NU:
+                        evac_first(hh)
+                        if hh % 4 >= 2:
+                            store(hh)
+                    if n % 4 == 2 and 0 <= n - 6 < NU:
+                        clip_first(n - 6)
+                        clip_first(n - 5)
+                    if n % 4 == 3 and 0 <= n - 7 < NU:
+                        clip_second(n - 7)
+                        clip_second(n - 6)
+                        store(n - 7)
+                        store(n - 6)
                     if 0 <= n - 1 < NU:
-                        regroup(n - 1)
-                if j == 1 and 0 <= n - 1 < NU:
-                    quantise(n - 1)
-                if j == 2 and 0 <= n - 4 < NU:
-                    evac_second(n - 4)
+                        quantise(n - 1)
                 if j == 3 and 0 <= n - 3 < NU:
                     stage2(n - 3)

from contextlib import ExitStack

import concourse.mybir as mybir
from concourse.masks import make_identity

F32 = mybir.dt.float32
BF16 = mybir.dt.bfloat16
U32 = mybir.dt.uint32
U8 = mybir.dt.uint8
FP8X4 = mybir.dt.float8_e4m3fn_x4
ACT = mybir.ActivationFunctionType
ALU = mybir.AluOpType

P = 128
B, G, S, H, K, E = 256, 16, 256, 1024, 256, 2
EPS = 1e-5
FLOPS = 2 * B * G * S * H * E + 2 * B * G * H * K * E

PIN = False
SPREAD = True
FULL = [(rg, e, (0, 1)) for rg in range(8) for e in range(2)]
GROUPS = FULL[:-1] + [(7, 1, (0,)), (7, 1, (1,))] if False else FULL
NG = len(GROUPS)
NU = 2 * NG
LE_CHUNKS = ((0, 2), (2, 4), (4, 8), (8, 16))


def on_vector(n, j):
    return (n == 0 and j % 2 == 1) or (n > 0 and j == 0 and n % 4 < 2)


def copy_engine(hh):
    return "v"


LE_ENG = "s"
W2_ENG = "v"


def tile_tgnetworkbias_pa_t_kernel(tc, le, ew1, ew2, ebg, ebb, ebm, ebv, out_0, out_1):
    nc = tc.nc
    with ExitStack() as ctx:
        const = ctx.enter_context(tc.tile_pool(name="const", bufs=1))
        hbp = ctx.enter_context(tc.tile_pool(name="hbp", bufs=3))
        grp = ctx.enter_context(tc.tile_pool(name="grp", bufs=3))
        cdp = ctx.enter_context(tc.tile_pool(name="cdp", bufs=8))
        outp = ctx.enter_context(tc.tile_pool(name="outp", bufs=8))
        ps1 = ctx.enter_context(tc.psum_pool(name="ps1", bufs=6))
        ps2 = ctx.enter_context(tc.psum_pool(name="ps2", bufs=2))

        if PIN:
            ctx.enter_context(tc.manual_schedule())

        le_v = le.rearrange("(bh p) g s -> p bh (g s)", p=P)
        le_raw = {}

        def load_le(q, ci):
            g0, g1 = LE_CHUNKS[ci]
            t = const.tile([P, 2 * (g1 - g0) * S], BF16, name="leraw%d" % ci)
            q.dma_start(out=t[:].rearrange("p (bh x) -> p bh x", bh=2), in_=le_v[:, :, g0 * S:g1 * S])
            le_raw[ci] = t

        w1raw = {}

        def load_w1(q, e, c):
            t = const.tile([P, 1024], BF16, name="w1raw%d%d" % (e, c))
            v = ew1[e].rearrange("(cu p e2) s -> p cu (e2 s)", cu=4, p=P, e2=2)
            q.dma_start(out=t[:].rearrange("p (u x) -> p u x", u=2), in_=v[:, 2 * c:2 * c + 2, :])
            w1raw[(e, c)] = t

        w2raw = {}

        def load_w2(q, e):
            t = const.tile([P, 2048], BF16, name="w2raw%d" % e)
            q.dma_start(out=t[:].rearrange("p (kb h) -> p kb h", kb=2),
                        in_=ew2[e].rearrange("(kb p) h -> p kb h", p=P))
            w2raw[e] = t

        load_le(nc.scalar, 0)
        load_w1(nc.scalar, 0, 0)
        load_w1(nc.scalar, 0, 1)
        bn_raw = []
        for i, src in enumerate((ebv, ebg, ebm, ebb)):
            t = const.tile([P, 256], BF16, name="bnraw%d" % i)
            nc.sync.dma_start(out=t[:], in_=src.rearrange("e g (cu x) -> (e g cu) x", x=256))
            bn_raw.append(t)
        ebv_sb, ebg_sb, ebm_sb, ebb_sb = bn_raw
        load_w1(nc.sync, 1, 0)
        load_w1(nc.sync, 1, 1)
        load_w2(nc.sync, 0)
        load_le(nc.sync, 1)
        load_w2(nc.sync, 1)
        load_le(nc.sync, 2)
        load_le(nc.sync, 3)

        ident = const.tile([P, P], F32, name="ident")
        make_identity(nc, ident[:])

        eps_t = const.tile([P, 1], F32, name="eps_t")
        nc.vector.memset(eps_t[:], EPS)
        warm = const.tile([P, 1], F32, name="warm")
        nc.scalar.activation(out=warm[:], in_=eps_t[:], func=ACT.Abs_reciprocal_sqrt)
        r = const.tile([P, 256], F32, name="r")
        nc.scalar.activation(out=r[:], in_=ebv_sb[:], func=ACT.Abs_reciprocal_sqrt, bias=eps_t[:, 0:1], scale=1.0)
        hv = const.tile([P, 256], F32, name="hv")
        nc.vector.tensor_scalar(out=hv[:], in0=ebv_sb[:], scalar1=EPS, scalar2=-0.5, op0=ALU.add, op1=ALU.mult)
        w = const.tile([P, 256], F32, name="w")
        for it in range(2):
            nc.vector.tensor_tensor(out=w[:], in0=r[:], in1=hv[:], op=ALU.mult)
            nc.vector.tensor_tensor(out=w[:], in0=w[:], in1=r[:], op=ALU.mult)
            nc.vector.scalar_tensor_tensor(out=r[:], in0=w[:], scalar=1.5, in1=r[:], op0=ALU.add, op1=ALU.mult)
        gs = const.tile([P, 512], F32, name="gs")
        nc.vector.tensor_tensor(out=gs[:, 0:256], in0=ebg_sb[:], in1=r[:], op=ALU.mult)
        nc.vector.tensor_tensor(out=w[:], in0=ebm_sb[:], in1=gs[:, 0:256], op=ALU.mult)
        nc.vector.tensor_tensor(out=gs[:, 256:512], in0=ebb_sb[:], in1=w[:], op=ALU.subtract)
        prm = const.tile([P, 512], F32, name="prm")

        def copy_out(eng, dst, srcv):
            if eng == "s":
                nc.scalar.copy(out=dst, in_=srcv)
            else:
                nc.vector.tensor_copy(out=dst, in_=srcv)

        jobs = []
        cursor = {"next": 0}

        def run_one_step():
            if cursor["next"] < len(jobs):
                jobs[cursor["next"]]()
                cursor["next"] = cursor["next"] + 1

        def flush_steps():
            for k in range(len(jobs) - cursor["next"]):
                run_one_step()

        def add_job(sources, finish):
            box = {}

            def step(i):
                if i == 0:
                    pt_new = ps1.tile([P, 512], F32, name="u")
                    box["pt"] = pt_new
                nc.tensor.transpose(box["pt"][:, i * P:(i + 1) * P], sources[i], ident[:])
                if i == 3:
                    finish(box["pt"])

            for i in range(4):
                jobs.append(lambda i=i: step(i))

        def prm_transposes():
            gv = gs[:].rearrange("p (k x e2) -> p k e2 x", k=2, e2=2)
            add_job([gv[:, kind, e2, :] for kind in range(2) for e2 in range(2)],
                    lambda pt: nc.vector.tensor_copy(out=prm[:], in_=pt[:]))

        leT = {}

        def le_transposes(rg, eng):
            ci = [i for i, (g0, g1) in enumerate(LE_CHUNKS) if g0 <= 2 * rg < g1][0]
            g0, g1 = LE_CHUNKS[ci]
            words = le_raw[ci][:].bitcast(F32)
            offs = [(bh * (g1 - g0) + 2 * rg + gi - g0) * P for gi in range(2) for bh in range(2)]
            t = const.tile([P, 512], F32, name="leT%d" % rg)
            add_job([words[:, o:o + P] for o in offs], lambda pt: copy_out(eng, t[:], pt[:]))
            leT[rg] = t

        w1T = {}

        def w1_transposes(e, c, eng):
            words = w1raw[(e, c)][:].bitcast(F32)
            t = const.tile([P, 512], F32, name="w1T%d%d" % (e, c))
            add_job([words[:, j * P:(j + 1) * P] for j in range(4)], lambda pt: copy_out(eng, t[:], pt[:]))
            w1T[(e, c)] = t

        w2c = {}
        w2s = {}

        def w2_prepare(e, eng):
            words = w2raw[e][:].bitcast(F32)
            g2 = const.tile([P, 2048], BF16, name="w2g%d" % e, align_bytes=64)
            g2w = g2[:].bitcast(F32)
            cw = const.tile([P, 512], U32, name="w2c%d" % e, align_bytes=64)
            sw = const.tile([P, 512], U8, name="w2s%d" % e, align_bytes=64)

            def finish(c, pt):
                copy_out(eng, g2w[:, c * 512:(c + 1) * 512].rearrange("p (k u) -> p k u", u=2),
                         pt[:].rearrange("p (u k) -> p k u", u=2))
                if c == 1:
                    nc.vector.quantize_mx(out=cw[:].bitcast(FP8X4), scales=sw[:], in_=g2[:])

            for c in range(2):
                add_job([words[:, kb * 512 + c * 256 + u * P:kb * 512 + c * 256 + (u + 1) * P] for u in range(2) for kb in range(2)],
                        lambda pt, c=c: finish(c, pt))
            w2c[e] = cw
            w2s[e] = sw

        ups = {}
        hbs = {}
        grs = {}
        cds = {}
        o2s = {}
        sgs = {}

        def bank_pe(n, j):
            rg, e, gis = GROUPS[n // 2]
            c = n % 2
            wd = 256 * len(gis)
            u_ps = ps1.tile([P, 512], F32, name="u")
            wv = w1T[(e, c)][:].bitcast(BF16).rearrange("q (x a) -> q x a", a=2)
            xv = leT[rg][:].bitcast(BF16).rearrange("q (x a) -> q x a", a=2)
            for a in range(2):
                nc.tensor.matmul(u_ps[:, 0:wd], lhsT=wv[:, j * P:(j + 1) * P, a], rhs=xv[:, gis[0] * 256:gis[0] * 256 + wd, a],
                                 start=(a == 0), stop=(a == 1))
                if SPREAD:
                    run_one_step()
            ups[(n, j)] = u_ps

        def bank_bn(n, j):
            rg, e, gis = GROUPS[n // 2]
            c = n % 2
            wd = 256 * len(gis)
            if j == 0:
                hb_new = hbp.tile([P, 2048], BF16, name="hb")
                hbs[n] = hb_new
            hb = hbs[n]
            u_ps = ups[(n, j)]
            for i, gi in enumerate(gis):
                rho = e * 64 + (2 * rg + gi) * 4 + 2 * c + j // 2
                cs = (j % 2) * P + rho
                cb = (2 + j % 2) * P + rho
                dst = hb[:, j * wd + i * 256:j * wd + (i + 1) * 256]
                srcv = u_ps[:, i * 256:(i + 1) * 256]
                if on_vector(n, j):
                    nc.vector.tensor_scalar(out=dst, in0=srcv, scalar1=prm[:, cs:cs + 1], scalar2=prm[:, cb:cb + 1],
                                            op0=ALU.mult, op1=ALU.add)
                else:
                    nc.scalar.activation(out=dst, in_=srcv, func=ACT.Relu, bias=prm[:, cb:cb + 1], scale=prm[:, cs:cs + 1])

        def regroup(n):
            wd = 256 * len(GROUPS[n // 2][2])
            gr = grp.tile([P, 2048], BF16, name="gr", align_bytes=64)
            dst = gr[:, 0:4 * wd].rearrange("p (c i t) -> p c t i", i=4, t=4)
            srcv = hbs[n][:, 0:4 * wd].rearrange("p (t c i) -> p c t i", t=4, i=4)
            nc.vector.tensor_scalar_max(out=dst, in0=srcv, scalar1=0.0)
            grs[n] = gr

        def quantise(n):
            cd = cdp.tile([P, 512], U32, name="cd", align_bytes=64)
            sc = cdp.tile([P, 512], U8, name="sc", align_bytes=64)
            wd = 256 * len(GROUPS[n // 2][2])
            nc.vector.quantize_mx(out=cd[:, 0:wd].bitcast(FP8X4), scales=sc[:, 0:wd], in_=grs[n][:, 0:4 * wd])
            cds[n] = (cd, sc)

        def stage2(hh):
            su, bh = hh // 2, hh % 2
            rg, e, gis = GROUPS[su]
            o2 = ps2.tile([P, 512], F32, name="o2")
            for gi in range(len(gis)):
                for c in range(2):
                    cd, sc = cds[2 * su + c]
                    cols = slice(gi * 256 + bh * P, gi * 256 + (bh + 1) * P)
                    nc.tensor.matmul_mx(
                        out=o2[:, gi * 256:(gi + 1) * 256],
                        lhsT=cd[:, cols].bitcast(FP8X4), lhsT_scale=sc[:, cols],
                        rhs=w2c[e][:, c * 256:(c + 1) * 256].bitcast(FP8X4), rhs_scale=w2s[e][:, c * 256:(c + 1) * 256],
                        start=(c == 0), stop=(c == 1))
            o2s[hh] = o2

        out_v = [o.rearrange("(bh p) g k -> p bh (g k)", p=P) for o in (out_0, out_1)]

        def evac_first(hh):
            sg = outp.tile([P, 512], F32, name="sg")
            rg, e, gis = GROUPS[hh // 2]
            wd = 256 * len(gis)
            if e == 0:
                nc.scalar.activation(out=sg[:, 0:wd], in_=o2s[hh][:, 0:wd], func=ACT.Sigmoid)
            else:
                copy_out(copy_engine(hh), sg[:, 0:wd], o2s[hh][:, 0:wd])
            sgs[hh] = sg

        def clip_first(hh):
            sg = sgs[hh]
            nc.vector.tensor_scalar(out=sg[:], in0=sg[:], scalar1=1.2, scalar2=-0.1, op0=ALU.mult, op1=ALU.add)

        def clip_second(hh):
            sg = sgs[hh]
            nc.vector.tensor_scalar(out=sg[:], in0=sg[:], scalar1=0.0, scalar2=1.0, op0=ALU.max, op1=ALU.min)

        def store(hh):
            su, bh = hh // 2, hh % 2
            rg, e, gis = GROUPS[su]
            wd = 256 * len(gis)
            o = rg * 512 + gis[0] * 256
            nc.sync.dma_start(out=out_v[e][:, bh, o:o + wd], in_=sgs[hh][:, 0:wd])

        le_transposes(0, "s")
        w1_transposes(0, 0, "s")
        flush_steps()
        w1_transposes(0, 1, "s")
        prm_transposes()
        if not SPREAD:
            bank_pe(0, 0)
            bank_pe(0, 1)
            flush_steps()
            bank_pe(0, 2)
            bank_pe(0, 3)
        else:
            for j in range(4):
                bank_pe(0, j)
        nc.scalar.activation(out=warm[:], in_=eps_t[:], func=ACT.Sigmoid)
        for j in range(4):
            bank_bn(0, j)

        for n in range(NU + 8):
            for j in range(4):
                if SPREAD:
                    if (n, j) == (1, 0):
                        w1_transposes(1, 0, "s")
                        w1_transposes(1, 1, "s")
                    if (n, j) == (2, 0):
                        w2_prepare(0, W2_ENG)
                    if (n, j) == (3, 0):
                        le_transposes(1, LE_ENG)
                    if (n, j) == (4, 0):
                        w2_prepare(1, W2_ENG)
                    if j == 0 and n % 4 == 1 and 2 <= n // 4 + 1 < 8 and n < 32:
                        le_transposes(n // 4 + 1, LE_ENG)
                else:
                    if (n, j) == (1, 2):
                        w1_transposes(1, 0, "s")
                        w1_transposes(1, 1, "s")
                    if (n, j) == (2, 2):
                        w2_prepare(0, W2_ENG)
                    if (n, j) == (4, 2):
                        w2_prepare(1, W2_ENG)
                    if j == 0 and n % 4 == 1 and n // 4 + 1 < 8 and n < 32:
                        le_transposes(n // 4 + 1, LE_ENG)
                    flush_steps()
                if j == 0 and 0 <= n - 1 < NU:
                    regroup(n - 1)
                if 1 <= n < NU:
                    bank_pe(n, j)
                    bank_bn(n, j)
                if j == 0:
                    hh = n - 4
                    if 0 <= hh < NU:
                        evac_first(hh)
                        if hh % 4 >= 2:
                            store(hh)
                    if n % 4 == 2 and 0 <= n - 6 < NU:
                        clip_first(n - 6)
                        clip_first(n - 5)
                    if n % 4 == 3 and 0 <= n - 7 < NU:
                        clip_second(n - 7)
                        clip_second(n - 6)
                        store(n - 7)
                        store(n - 6)
                    if 0 <= n - 1 < NU:
                        quantise(n - 1)
                if j == 3 and 0 <= n - 3 < NU:
                    stage2(n - 3)
